import numpy as np
import ml_dtypes


def mxq(x, axis, fmt="e4m3"):
    dtype, down = {"e4m3": (ml_dtypes.float8_e4m3fn, 7), "e5m2": (ml_dtypes.float8_e5m2, 14)}[fmt]
    v = np.moveaxis(np.asarray(x, np.float32).astype(ml_dtypes.bfloat16).astype(np.float64), axis, -1)
    blocks = v.reshape(v.shape[:-1] + (-1, 32))
    amax = np.abs(blocks).max(-1, keepdims=True)
    byte = np.maximum(np.where(amax > 0, np.frexp(amax)[1] - 1 + 127, 0) - down, 1)
    scale = np.exp2(byte - 127.0)
    codes = (blocks / scale).astype(np.float32).astype(dtype).astype(np.float64)
    return np.moveaxis((codes * scale).reshape(v.shape), -1, axis)


WIDE = False


def mx_kscale(k):
    if not WIDE:
        return np.ones(k)
    levels = np.array([10, -10, 5, -5, 0])
    if k % 512:
        return np.exp2(np.random.permutation(np.resize(levels, k // 32))).repeat(32)
    a = np.empty((k // 512, 16))
    for p in range(k // 512):
        a[p, :8] = np.random.permutation(np.resize(levels, 8))
        for g in range(8):
            far = levels[np.abs(levels - a[p, g]) >= 10]
            a[p, g + 8] = far[np.random.randint(len(far))]
    return np.exp2(a.ravel()).repeat(32)


BF16 = ml_dtypes.bfloat16


def bf(x):
    return np.asarray(x, np.float32).astype(BF16)


def f64(x):
    return np.asarray(x).astype(np.float64)


B, S, E, H, KVH, D = 1, 512, 2048, 16, 4, 128


def rope(t, cos, sin):
    tr = t.reshape(t.shape[:-1] + (-1, 2))
    xr, xi = tr[..., 0], tr[..., 1]
    c = cos[None, :, None, :]
    n = sin[None, :, None, :]
    return np.stack([xr * c - xi * n, xr * n + xi * c], axis=-1).reshape(t.shape)


def draw0():
    s = mx_kscale(E)
    a = np.sqrt(2.0 / E)
    ang = np.outer(np.arange(S), 1.0 / (10000.0 ** (np.arange(0, D, 2) / D)))
    return {"x": bf(np.random.standard_normal((B, S, E)) * s),
            "wq_w": bf(np.random.standard_normal((H * D, E)) * a / s[None, :]),
            "wk_w": bf(np.random.standard_normal((KVH * D, E)) * a / s[None, :]),
            "wv_w": bf(np.random.standard_normal((KVH * D, E)) * a / s[None, :]),
            "freqs_cos": bf(np.cos(ang)), "freqs_sin": bf(np.sin(ang))}


def core(x, wq_w, wk_w, wv_w, freqs_cos, freqs_sin):
    xq = mxq(f64(x), 2, "e4m3")
    q = (xq @ mxq(f64(wq_w), 1, "e4m3").T).reshape(B, S, H, D)
    k = (xq @ mxq(f64(wk_w), 1, "e4m3").T).reshape(B, S, KVH, D)
    v = (xq @ mxq(f64(wv_w), 1, "e4m3").T).reshape(B, S, KVH, D)
    c, n = f64(freqs_cos), f64(freqs_sin)
    return rope(q, c, n), rope(k, c, n), v


def e4m3fn_bytes(y):
    return np.clip(np.asarray(y, np.float64), -448.0, 448.0).astype(np.float32).astype(ml_dtypes.float8_e4m3fn).view(np.uint8)


def e4m3fn_values(b):
    return np.asarray(b, np.uint8).view(ml_dtypes.float8_e4m3fn).astype(np.float64)


def setup_inputs():
    d = draw0()
    x0 = np.asarray(d['wq_w']).astype(np.float64)
    s = (np.max(np.abs(x0), axis=(0,), keepdims=True) / 448.0).astype(np.float32)
    out = {}
    for k, v in d.items():
        if k == 'wq_w':
            out['wq_w_bytes'] = e4m3fn_bytes(x0 / s.astype(np.float64))
            out['wq_w_scale'] = s
        else:
            out[k] = v
    return out


def reference(x, wq_w_bytes, wq_w_scale, wk_w, wv_w, freqs_cos, freqs_sin):
    return core(x, e4m3fn_values(wq_w_bytes) * wq_w_scale.astype(np.float64), wk_w, wv_w, freqs_cos, freqs_sin)

@@ -1,0 +1,402 @@
+from contextlib import ExitStack
+
+import concourse.mybir as mybir
+from concourse.masks import make_identity
+
+F32 = mybir.dt.float32
+BF16 = mybir.dt.bfloat16
+U8 = mybir.dt.uint8
+U32 = mybir.dt.uint32
+FP8 = mybir.dt.float8_e4m3fn
+FP8X4 = mybir.dt.float8_e4m3fn_x4
+MULT = mybir.AluOpType.mult
+ADD = mybir.AluOpType.add
+COPY = mybir.ActivationFunctionType.Copy
+
+P = 128
+E = 2048
+PASSES = 4
+FLOPS = 2 * 512 * 3072 * 2048
+
+T_ORDER = (0, 24, 1, 25, 2, 26, 3, 27, 4, 5, 6, 7, 16, 17, 12, 13, 18, 19, 8, 9, 14, 15, 20, 21, 10, 11, 22, 23)
+M_ORDER = (0, 1, 2, 8, 3, 9, 6, 4, 10, 7, 5, 11)
+SCALED = (6, 7)
+LEAD = 2
+LEAD_HEAD = 2
+Q_LAG = 3
+Q_LAG_HEAD = 3
+Q_LAG_SCALED = 2
+ROPE_LAG = 3
+BURST = 1
+POOL_ADDS = True
+WARM0 = 14
+WARM1 = 2
+WARM_EVERY = 3
+CAST_FROM = 6
+MM_BURST = 1
+DEFER = True
+LOAD_ORDER = (0, 'sc', 1, 2, 24, 3, 25, 4, 26, 5, 6, 'cs', 27, 7, 12, 13, 16, 8, 17, 9, 14, 15, 18, 10, 19, 11)
+LATE_LOADS = (20, 21, 22, 23)
+
+
+def schedule(t_order, m_order, scaled, lead, q_lag, q_lag_scaled, rope_lag, burst, pool_adds, warm0, warm1, cast_from, load_order, late_loads, mm_burst=1, defer=False, warm_every=1, pair_rope=False, q_lag_head=None, lead_head=None):
+    ops = []
+    for t in load_order:
+        ops.append(("load", t))
+    if warm0:
+        ops.append(("dummy", warm0))
+    banks = [(pr, mp) for pr in m_order for mp in (0, 1)]
+    last_turn = {}
+    for s, t in enumerate(t_order):
+        last_turn[t // 2] = s
+    casts = [(t, h) for t in t_order if t // 2 in scaled for h in (0, 1)]
+    n_cast = 0
+    weaves = []
+    n_weave = 0
+    products = [t for t in t_order if t < 16 and t // 2 not in scaled]
+    n_made = 0
+    q_order = [12, m_order[0], 13] + list(m_order[1:])
+    n_q = 0
+    quantized = set()
+    n_mm = 0
+    mm_step = {}
+    n_rope = 0
+    steps = len(t_order)
+    s = 0
+    while n_rope < len(banks):
+        assert s < 200
+        want = n_cast + 1 if s >= cast_from else n_cast
+        if s < steps and t_order[s] // 2 in scaled:
+            want = max(want, 1 + max(i for i in range(len(casts)) if casts[i][0] // 2 == t_order[s] // 2))
+        want = min(want, len(casts))
+        if n_weave < len(weaves) and n_cast >= want:
+            ops.append(("weave",) + weaves[n_weave])
+            n_weave += 1
+        while n_cast < want:
+            ops.append(("cast",) + casts[n_cast])
+            n_cast += 1
+        turned = len([t for t in products if t in t_order[: s + 1]])
+        ahead = lead_head if (lead_head is not None and n_mm == 0) else lead
+        while n_made < min(turned + ahead, len(products)):
+            ops.append(("product", products[n_made], 1 if n_made else 4))
+            n_made += 1
+        if s < steps:
+            t = t_order[s]
+            if t // 2 in scaled:
+                for g in (2 * (t % 2), 2 * (t % 2) + 1):
+                    ops.append(("turn_scaled", t // 2, g))
+                    if defer:
+                        weaves.append((t // 2, g))
+                    else:
+                        ops.append(("weave", t // 2, g))
+            else:
+                ops.append(("turn", t))
+                if t == 27:
+                    for late in late_loads:
+                        ops.append(("load", late))
+            if warm1 and n_mm == 0 and s % warm_every == warm_every - 1:
+                ops.append(("dummy", warm1))
+        due = [b for b in range(n_rope, n_mm) if mm_step[b] + rope_lag <= s]
+        if pair_rope:
+            while len(due) >= 2:
+                pr = banks[due[0]][0]
+                if pr >= 10:
+                    ops.append(("evac", pr, 0))
+                    ops.append(("evac", pr, 1))
+                else:
+                    ops.append(("rope_pair", pr, pool_adds))
+                n_rope += 2
+                due = due[2:]
+        elif len(due) >= burst or (n_mm == len(banks) and due):
+            for b in due:
+                pr, mp = banks[b]
+                if pr >= 10:
+                    ops.append(("evac", pr, mp))
+                else:
+                    ops.append(("rope", pr, mp, pool_adds and b != due[-1]))
+                n_rope += 1
+        if n_q < len(q_order):
+            pr = q_order[n_q]
+            lag = q_lag_scaled if pr in scaled else q_lag
+            if q_lag_head is not None and n_q < 3:
+                lag = q_lag_head
+            if last_turn[pr] + lag <= s and (pr, 3) not in weaves[n_weave:]:
+                ops.append(("quantize", pr))
+                quantized.add(pr)
+                n_q += 1
+        ready = 0
+        while n_mm + ready < len(banks) and ready < mm_burst:
+            pr, mp = banks[n_mm + ready]
+            if pr in quantized and 12 + mp in quantized and n_rope > n_mm + ready - 4:
+                ready += 1
+            else:
+                break
+        if ready == mm_burst or (s >= steps and ready) or n_mm + ready == len(banks):
+            for i in range(ready):
+                ops.append(("mm",) + banks[n_mm])
+                mm_step[n_mm] = s
+                n_mm += 1
+        s += 1
+    ops.append(("flush",))
+    return ops
+
+
+def tile_attention_pa_kernel(
+    tc, x, wq_w_bytes, wq_w_scale, wk_w, wv_w, freqs_cos, freqs_sin, out_0, out_1, out_2
+):
+    nc = tc.nc
+    x_rows = x.flatten_outer_dims()
+    scale_row = wq_w_scale.rearrange("o k -> (o k)")
+    out_views = (
+        out_0.rearrange("b (m p) h d -> p (b m) (h d)", p=P),
+        out_1.rearrange("b (m p) h d -> p (b m) (h d)", p=P),
+        out_2.rearrange("b (m p) h d -> p (b m) (h d)", p=P),
+    )
+
+    with ExitStack() as ctx:
+        const = ctx.enter_context(tc.tile_pool(name="const", bufs=1))
+        bytes_pool = ctx.enter_context(tc.tile_pool(name="bytesp", bufs=1))
+        raw = ctx.enter_context(tc.tile_pool(name="raw", bufs=1))
+        wbf_pool = ctx.enter_context(tc.tile_pool(name="wbfp", bufs=max(LEAD, LEAD_HEAD) + 3))
+        plane_pool = ctx.enter_context(tc.tile_pool(name="planep", bufs=5))
+        grp_pool = ctx.enter_context(tc.tile_pool(name="grpp", bufs=5))
+        code_pool = ctx.enter_context(tc.tile_pool(name="codep", bufs=1))
+        work = ctx.enter_context(tc.tile_pool(name="work", bufs=2))
+        psum = ctx.enter_context(tc.psum_pool(name="psum", bufs=1))
+        ctx.enter_context(tc.manual_schedule())
+
+        zeros = const.tile([P, 512], BF16, name="zeros")
+        nc.vector.memset(zeros[:], 0.0)
+        warm = const.tile([P, 2], F32, name="warm")
+        nc.vector.memset(warm[:, 0:1], 0.0)
+        nc.scalar.activation(out=warm[:, 1:2], in_=warm[:, 0:1], func=COPY, scale=1.0)
+        ident = const.tile([P, P], F32, name="ident")
+        make_identity(nc, ident[:])
+
+        scale_bc = const.tile([P, E], F32, name="scale_bc")
+        scale_col = const.tile([P, PASSES, 4], F32, name="scale_col")
+        cos_t = const.tile([P, 4, 64], BF16, name="cos_t")
+        sin_t = const.tile([P, 4, 64], BF16, name="sin_t")
+        cos3 = const.tile([P, 4, 2, 64, 2], BF16, name="cos3")
+        sin3 = const.tile([P, 4, 2, 2, 64], BF16, name="sin3")
+        wq_codes_in = {}
+        words = {}
+
+        def load(t):
+            if t == "sc":
+                for c in range(4):
+                    nc.sync.dma_start(
+                        out=scale_bc[:, c * 512 : (c + 1) * 512],
+                        in_=scale_row[c * 512 : (c + 1) * 512].partition_broadcast(P),
+                    )
+            elif t == "cs":
+                nc.sync.dma_start(out=cos_t[:], in_=freqs_cos.rearrange("(m p) j -> p m j", p=P))
+                nc.sync.dma_start(out=sin_t[:], in_=freqs_sin.rearrange("(m p) j -> p m j", p=P))
+                nc.sync.dma_start(out=scale_col[:], in_=wq_w_scale.rearrange("o (g p t) -> p (o g) t", p=P, t=4))
+                for h in range(2):
+                    nc.gpsimd.tensor_copy(out=cos3[:, :, h, :, :], in_=cos_t[:].unsqueeze(3).to_broadcast([P, 4, 64, 2]))
+                    nc.gpsimd.tensor_copy(out=sin3[:, :, 0, h, :], in_=sin_t[:])
+                    nc.gpsimd.tensor_scalar(
+                        out=sin3[:, :, 1, h, :], in0=sin_t[:], scalar1=-1.0, scalar2=0.0, op0=MULT, op1=ADD
+                    )
+            elif t < 16:
+                b = bytes_pool.tile([P, E], U8, name="wq_bytes_%d" % t)
+                nc.sync.dma_start(out=b[:], in_=wq_w_bytes[t * P : (t + 1) * P, :])
+                wq_codes_in[t] = b
+            else:
+                src = (wk_w, wv_w, x_rows)[(t - 16) // 4]
+                j = t % 4
+                rows = raw.tile([P, E], BF16, name="rows_%d" % t, tag=("rk%d" % j) if t < 20 else ("rx%d" % j))
+                nc.sync.dma_start(out=rows[:], in_=src[j * P : (j + 1) * P, :])
+                words[t] = rows[:].bitcast(F32)
+
+        pend = []
+        flushed = [0]
+
+        def tick():
+            if flushed[0] < len(pend):
+                flushed[0] = flushed[0] + 1
+                pend[flushed[0] - 1]()
+
+        dummy_out = []
+
+        def dummy(n):
+            if not dummy_out:
+                dummy_out.append(psum.tile([P, 512], F32, name="dummy_out", tag="b3"))
+            for i in range(n):
+                nc.tensor.matmul(dummy_out[0][:], lhsT=zeros[:, 0:P], rhs=zeros[:], start=True, stop=True)
+
+        def product(t, chunks):
+            w = wbf_pool.tile([P, E], BF16, name="wbf_%d" % t, tag="wbf")
+            n = E // chunks
+            for c in range(chunks):
+                cs = slice(c * n, (c + 1) * n)
+                nc.vector.tensor_tensor(
+                    out=w[:, cs], in0=wq_codes_in[t][:, cs].bitcast(FP8), in1=scale_bc[:, cs], op=MULT
+                )
+            words[t] = w[:].bitcast(F32)
+            tick()
+
+        cast_tiles = {}
+
+        def cast(t, h):
+            if t not in cast_tiles:
+                cast_tiles[t] = raw.tile([P, E], BF16, name="wcast_%d" % t)
+                words[t] = cast_tiles[t][:].bitcast(F32)
+            cs = slice(h * 1024, (h + 1) * 1024)
+            nc.scalar.copy(out=cast_tiles[t][:, cs], in_=wq_codes_in[t][:, cs].bitcast(FP8))
+
+        grp = {}
+        n_tbank = [0]
+
+        def tbank(shape, name):
+            n_tbank[0] = n_tbank[0] + 1
+            return psum.tile(shape, F32, name=name, tag="b%d" % (4 + (n_tbank[0] - 1) % 4))
+
+        def grp_tile(pair):
+            if pair not in grp:
+                grp[pair] = grp_pool.tile([P, PASSES, 2 * P, 4], BF16, name="grp_%d" % pair, tag="grp", align_bytes=64)
+            return grp[pair]
+
+        def turn(t):
+            pair, i = t // 2, t % 2
+            grp_words = grp_tile(pair)[:].bitcast(F32)
+            for gg in range(2):
+                tp = tbank([P, 2, 2, P], "tp_%d_%d" % (t, gg))
+                for g2 in range(2):
+                    g = 2 * gg + g2
+                    for u in range(2):
+                        nc.tensor.transpose(tp[:, g2, u, :], words[t][:, 256 * g + u : 256 * (g + 1) : 2], ident[:])
+                nc.scalar.copy(
+                    out=grp_words[:, 2 * gg : 2 * gg + 2, i * P : (i + 1) * P, :],
+                    in_=tp[:].rearrange("p g u r -> p g r u"),
+                )
+
+        plane_tiles = {}
+
+        def turn_scaled(pair, g):
+            grp_tile(pair)
+            tp = tbank([P, 2, 2 * P], "tps_%d_%d" % (pair, g))
+            for i in range(2):
+                for u in range(2):
+                    nc.tensor.transpose(
+                        tp[:, u, i * P : (i + 1) * P], words[2 * pair + i][:, 256 * g + u : 256 * (g + 1) : 2], ident[:]
+                    )
+            halves = tp[:].rearrange("p u c -> p (u c)").bitcast(BF16).rearrange("p (u c e) -> p u c e", u=2, e=2)
+            planes = plane_pool.tile([P, 4, 2 * P], BF16, name="planes_%d_%d" % (pair, g), tag="planes")
+            for t in range(4):
+                nc.scalar.activation(
+                    out=planes[:, t, :], in_=halves[:, t // 2, :, t % 2], func=COPY, scale=scale_col[:, g, t : t + 1]
+                )
+            plane_tiles[(pair, g)] = planes
+
+        def weave(pair, g):
+            nc.scalar.copy(out=grp[pair][:, g, :, :], in_=plane_tiles[(pair, g)][:].rearrange("p t c -> p c t"))
+
+        codes = {}
+        scales = {}
+
+        def quantize(pair):
+            if pair < 12:
+                c = code_pool.tile([P, 1024], U32, name="codes_%d" % pair, tag="wc", bufs=4, align_bytes=64)
+                s = code_pool.tile([P, 1024], U8, name="scales_%d" % pair, tag="ws", bufs=4, align_bytes=64)
+            else:
+                c = code_pool.tile([P, 1024], U32, name="codes_%d" % pair, align_bytes=64)
+                s = code_pool.tile([P, 1024], U8, name="scales_%d" % pair, align_bytes=64)
+            nc.vector.quantize_mx(
+                out=c[:].bitcast(FP8X4), scales=s[:], in_=grp[pair][:].rearrange("p g c t -> p (g c t)")
+            )
+            codes[pair] = c
+            scales[pair] = s
+            tick()
+
+        acc = {}
+        n_acc = [0]
+
+        def mm(pair, mp):
+            a = psum.tile([P, 2, 256], F32, name="acc_%d_%d" % (pair, mp), tag="b%d" % (n_acc[0] % 4))
+            n_acc[0] = n_acc[0] + 1
+            acc[(pair, mp)] = a
+            for mh in range(2):
+                for g in range(PASSES):
+                    xs = slice(g * 256 + mh * P, g * 256 + mh * P + P)
+                    ws = slice(g * 256, (g + 1) * 256)
+                    nc.tensor.matmul_mx(
+                        out=a[:, mh, :],
+                        lhsT=codes[12 + mp][:, xs].bitcast(FP8X4),
+                        lhsT_scale=scales[12 + mp][:, xs],
+                        rhs=codes[pair][:, ws].bitcast(FP8X4),
+                        rhs_scale=scales[pair][:, ws],
+                        start=(g == 0),
+                        stop=(g == PASSES - 1),
+                    )
+
+        def store(pair, mp, tile2):
+            view = out_views[0] if pair < 8 else out_views[1] if pair < 10 else out_views[2]
+            col = (pair if pair < 8 else pair % 2) * 256
+            nc.sync.dma_start(out=view[:, 2 * mp : 2 * mp + 2, col : col + 256], in_=tile2)
+
+        def rope_pair(pair, on_pool):
+            ta = work.tile([P, 4, 256], F32, name="ta_%d" % pair, tag="ta")
+            tb = work.tile([P, 4, 2, P], F32, name="tb_%d" % pair, tag="tb")
+            r = work.tile([P, 4, 256], F32, name="r_%d" % pair, tag="r")
+            view = out_views[0] if pair < 8 else out_views[1]
+            col = (pair if pair < 8 else pair % 2) * 256
+
+            def add(eng, m0, m1):
+                eng.tensor_tensor(
+                    out=r[:, m0:m1, :].rearrange("p m (q e) -> p m q e", e=2),
+                    in0=ta[:, m0:m1, :].rearrange("p m (q e) -> p m q e", e=2),
+                    in1=tb[:, m0:m1, ::-1, :].rearrange("p m e q -> p m q e"),
+                    op=ADD,
+                )
+                nc.sync.dma_start(out=view[:, m0:m1, col : col + 256], in_=r[:, m0:m1, :])
+
+            for mp in range(2):
+                a = acc[(pair, mp)]
+                ms = slice(2 * mp, 2 * mp + 2)
+                nc.vector.tensor_tensor(
+                    out=ta[:, ms, :],
+                    in0=a[:],
+                    in1=cos3[:, ms, :, :, :].rearrange("p m h j e -> p m (h j e)"),
+                    op=MULT,
+                )
+                if mp == 0:
+                    tick()
+                nc.vector.tensor_tensor(
+                    out=tb[:, ms, :, :],
+                    in0=a[:].rearrange("p m (q e) -> p m e q", e=2),
+                    in1=sin3[:, ms, :, :, :].rearrange("p m e h j -> p m e (h j)"),
+                    op=MULT,
+                )
+                if on_pool and mp == 0:
+                    add(nc.gpsimd, 0, 1)
+
+            def rest():
+                add(nc.vector, 1 if on_pool else 0, 4)
+
+            pend.append(rest)
+
+        def evac(pair, mp):
+            vt = work.tile([P, 2, 256], F32, name="vt_%d_%d" % (pair, mp), tag="vt")
+            nc.scalar.copy(out=vt[:], in_=acc[(pair, mp)][:])
+            store(pair, mp, vt[:])
+
+        run = {
+            "load": load,
+            "dummy": dummy,
+            "cast": cast,
+            "product": product,
+            "turn": turn,
+            "turn_scaled": turn_scaled,
+            "weave": weave,
+            "quantize": quantize,
+            "mm": mm,
+            "rope_pair": rope_pair,
+            "evac": evac,
+            "flush": tick,
+        }
+        for op in schedule(
+            T_ORDER, M_ORDER, SCALED, LEAD, Q_LAG, Q_LAG_SCALED, ROPE_LAG, BURST, POOL_ADDS, WARM0, WARM1, CAST_FROM, LOAD_ORDER, LATE_LOADS, MM_BURST, DEFER, WARM_EVERY, True, Q_LAG_HEAD, LEAD_HEAD
+        ):
+            run[op[0]](*op[1:])

@@ -18,10 +18,10 @@ E = 2048
 PASSES = 4
 FLOPS = 2 * 512 * 3072 * 2048
 
-T_ORDER = (0, 24, 1, 25, 2, 26, 3, 27, 4, 5, 6, 7, 16, 17, 12, 13, 18, 19, 8, 9, 14, 15, 20, 21, 10, 11, 22, 23)
-M_ORDER = (0, 1, 2, 8, 3, 9, 6, 4, 10, 7, 5, 11)
+T_ORDER = (0, 24, 1, 25, 2, 26, 3, 27, 4, 5, 6, 7, 16, 17, 12, 13, 18, 19, 8, 9, 14, 15, 20, 21, 22, 23, 10, 11)
+M_ORDER = (0, 1, 2, 8, 3, 9, 6, 4, 10, 7, 11, 5)
 SCALED = (6, 7)
-LEAD = 2
+LEAD = 1
 LEAD_HEAD = 2
 Q_LAG = 3
 Q_LAG_HEAD = 3
@@ -29,13 +29,20 @@ Q_LAG_SCALED = 2
 ROPE_LAG = 3
 BURST = 1
 POOL_ADDS = True
-WARM0 = 14
+POOL_OWN = 256
+POOL_LAST = 320
+SHARED = 8
+WARM0 = 12
+WARM_FIRST = 2
+TABLE_STEP = 0
 WARM1 = 2
 WARM_EVERY = 3
 CAST_FROM = 6
 MM_BURST = 1
+MM_LAG_HEAD = 1
+MM_HEAD = 4
 DEFER = True
-LOAD_ORDER = (0, 'sc', 1, 2, 24, 3, 25, 4, 26, 5, 6, 'cs', 27, 7, 12, 13, 16, 8, 17, 9, 14, 15, 18, 10, 19, 11)
+LOAD_ORDER = ('sc', 0, 1, 'cs', 2, 24, 3, 25, 4, 26, 5, 6, 27, 7, 12, 13, 16, 8, 17, 9, 14, 15, 18, 10, 19, 11)
 LATE_LOADS = (20, 21, 22, 23)
 
 
@@ -43,6 +50,8 @@ def schedule(t_order, m_order, scaled, lead, q_lag, q_lag_scaled, rope_lag, burs
     ops = []
     for t in load_order:
         ops.append(("load", t))
+    ops.append(("dummy", WARM_FIRST))
+    ops.append(("spread",))
     if warm0:
         ops.append(("dummy", warm0))
     banks = [(pr, mp) for pr in m_order for mp in (0, 1)]
@@ -57,7 +66,7 @@ def schedule(t_order, m_order, scaled, lead, q_lag, q_lag_scaled, rope_lag, burs
     n_made = 0
     q_order = [12, m_order[0], 13] + list(m_order[1:])
     n_q = 0
-    quantized = set()
+    quantized = {}
     n_mm = 0
     mm_step = {}
     n_rope = 0
@@ -80,6 +89,8 @@ def schedule(t_order, m_order, scaled, lead, q_lag, q_lag_scaled, rope_lag, burs
         while n_made < min(turned + ahead, len(products)):
             ops.append(("product", products[n_made], 1 if n_made else 4))
             n_made += 1
+        if s == TABLE_STEP:
+            ops.append(("tables",))
         if s < steps:
             t = t_order[s]
             if t // 2 in scaled:
@@ -122,12 +133,13 @@ def schedule(t_order, m_order, scaled, lead, q_lag, q_lag_scaled, rope_lag, burs
                 lag = q_lag_head
             if last_turn[pr] + lag <= s and (pr, 3) not in weaves[n_weave:]:
                 ops.append(("quantize", pr))
-                quantized.add(pr)
+                quantized[pr] = s
                 n_q += 1
         ready = 0
         while n_mm + ready < len(banks) and ready < mm_burst:
             pr, mp = banks[n_mm + ready]
-            if pr in quantized and 12 + mp in quantized and n_rope > n_mm + ready - 4:
+            wait = MM_LAG_HEAD if n_mm + ready < MM_HEAD else 0
+            if quantized.get(pr, 999) + wait <= s and quantized.get(12 + mp, 999) + wait <= s and n_rope > n_mm + ready - 4:
                 ready += 1
             else:
                 break
@@ -146,7 +158,6 @@ def tile_attention_pa_kernel(
 ):
     nc = tc.nc
     x_rows = x.flatten_outer_dims()
-    scale_row = wq_w_scale.rearrange("o k -> (o k)")
     out_views = (
         out_0.rearrange("b (m p) h d -> p (b m) (h d)", p=P),
         out_1.rearrange("b (m p) h d -> p (b m) (h d)", p=P),
@@ -177,28 +188,17 @@ def tile_attention_pa_kernel(
         scale_col = const.tile([P, PASSES, 4], F32, name="scale_col")
         cos_t = const.tile([P, 4, 64], BF16, name="cos_t")
         sin_t = const.tile([P, 4, 64], BF16, name="sin_t")
-        cos3 = const.tile([P, 4, 2, 64, 2], BF16, name="cos3")
-        sin3 = const.tile([P, 4, 2, 2, 64], BF16, name="sin3")
+        cos_n = const.tile([P, 4, 2, 64, 2], BF16, name="cos_n")
+        sin_n = const.tile([P, 4, 2, 64, 2], BF16, name="sin_n")
         wq_codes_in = {}
         words = {}
 
         def load(t):
             if t == "sc":
-                for c in range(4):
-                    nc.sync.dma_start(
-                        out=scale_bc[:, c * 512 : (c + 1) * 512],
-                        in_=scale_row[c * 512 : (c + 1) * 512].partition_broadcast(P),
-                    )
+                nc.sync.dma_start(out=scale_col[:], in_=wq_w_scale.rearrange("o (g p t) -> p (o g) t", p=P, t=4))
             elif t == "cs":
                 nc.sync.dma_start(out=cos_t[:], in_=freqs_cos.rearrange("(m p) j -> p m j", p=P))
                 nc.sync.dma_start(out=sin_t[:], in_=freqs_sin.rearrange("(m p) j -> p m j", p=P))
-                nc.sync.dma_start(out=scale_col[:], in_=wq_w_scale.rearrange("o (g p t) -> p (o g) t", p=P, t=4))
-                for h in range(2):
-                    nc.gpsimd.tensor_copy(out=cos3[:, :, h, :, :], in_=cos_t[:].unsqueeze(3).to_broadcast([P, 4, 64, 2]))
-                    nc.gpsimd.tensor_copy(out=sin3[:, :, 0, h, :], in_=sin_t[:])
-                    nc.gpsimd.tensor_scalar(
-                        out=sin3[:, :, 1, h, :], in0=sin_t[:], scalar1=-1.0, scalar2=0.0, op0=MULT, op1=ADD
-                    )
             elif t < 16:
                 b = bytes_pool.tile([P, E], U8, name="wq_bytes_%d" % t)
                 nc.sync.dma_start(out=b[:], in_=wq_w_bytes[t * P : (t + 1) * P, :])
@@ -210,13 +210,19 @@ def tile_attention_pa_kernel(
                 nc.sync.dma_start(out=rows[:], in_=src[j * P : (j + 1) * P, :])
                 words[t] = rows[:].bitcast(F32)
 
+        def tables():
+            for h in range(2):
+                nc.scalar.copy(out=cos_n[:, :, h, :, :], in_=cos_t[:].unsqueeze(3).to_broadcast([P, 4, 64, 2]))
+                nc.scalar.activation(out=sin_n[:, :, h, :, 0], in_=sin_t[:], func=COPY, scale=-1.0)
+                nc.scalar.copy(out=sin_n[:, :, h, :, 1], in_=sin_t[:])
+
         pend = []
         flushed = [0]
 
-        def tick():
+        def tick(last):
             if flushed[0] < len(pend):
                 flushed[0] = flushed[0] + 1
-                pend[flushed[0] - 1]()
+                pend[flushed[0] - 1](last)
 
         dummy_out = []
 
@@ -235,7 +241,6 @@ def tile_attention_pa_kernel(
                     out=w[:, cs], in0=wq_codes_in[t][:, cs].bitcast(FP8), in1=scale_bc[:, cs], op=MULT
                 )
             words[t] = w[:].bitcast(F32)
-            tick()
 
         cast_tiles = {}
 
@@ -270,6 +275,16 @@ def tile_attention_pa_kernel(
                 nc.scalar.copy(
                     out=grp_words[:, 2 * gg : 2 * gg + 2, i * P : (i + 1) * P, :],
                     in_=tp[:].rearrange("p g u r -> p g r u"),
+                )
+
+        def spread():
+            for g in range(PASSES):
+                sp = tbank([P, 4, P], "spread_%d" % g)
+                for t in range(4):
+                    nc.tensor.transpose(sp[:, t, :], scale_col[:, g, t : t + 1].to_broadcast([P, P]), ident[:])
+                nc.scalar.copy(
+                    out=scale_bc[:, g * 512 : (g + 1) * 512].rearrange("p (n t) -> p n t", t=4),
+                    in_=sp[:].rearrange("p t n -> p n t"),
                 )
 
         plane_tiles = {}
@@ -308,7 +323,6 @@ def tile_attention_pa_kernel(
             )
             codes[pair] = c
             scales[pair] = s
-            tick()
 
         acc = {}
         n_acc = [0]
@@ -337,43 +351,49 @@ def tile_attention_pa_kernel(
             nc.sync.dma_start(out=view[:, 2 * mp : 2 * mp + 2, col : col + 256], in_=tile2)
 
         def rope_pair(pair, on_pool):
-            ta = work.tile([P, 4, 256], F32, name="ta_%d" % pair, tag="ta")
-            tb = work.tile([P, 4, 2, P], F32, name="tb_%d" % pair, tag="tb")
-            r = work.tile([P, 4, 256], F32, name="r_%d" % pair, tag="r")
+            tick(False)
+            own = POOL_LAST if pair == [pr for pr in M_ORDER if pr < 10][-1] else POOL_OWN
+            ca = work.tile([P, 4, 256], F32, name="ca_%d" % pair, tag="ca")
+            sb = work.tile([P, 4, 256], F32, name="sb_%d" % pair, tag="sb")
+            r = work.tile([P, 4, 256], F32, name="r_%d" % pair, tag="r", bufs=3)
             view = out_views[0] if pair < 8 else out_views[1]
             col = (pair if pair < 8 else pair % 2) * 256
 
-            def add(eng, m0, m1):
+            def add(eng, c0, c1):
                 eng.tensor_tensor(
-                    out=r[:, m0:m1, :].rearrange("p m (q e) -> p m q e", e=2),
-                    in0=ta[:, m0:m1, :].rearrange("p m (q e) -> p m q e", e=2),
-                    in1=tb[:, m0:m1, ::-1, :].rearrange("p m e q -> p m q e"),
+                    out=r[:].rearrange("p m c -> p (m c)")[:, c0:c1],
+                    in0=ca[:].rearrange("p m c -> p (m c)")[:, c0:c1],
+                    in1=sb[:].rearrange("p m c -> p (m c)")[:, c0:c1],
                     op=ADD,
                 )
+
+            def store(m0, m1):
                 nc.sync.dma_start(out=view[:, m0:m1, col : col + 256], in_=r[:, m0:m1, :])
 
             for mp in range(2):
                 a = acc[(pair, mp)]
                 ms = slice(2 * mp, 2 * mp + 2)
                 nc.vector.tensor_tensor(
-                    out=ta[:, ms, :],
-                    in0=a[:],
-                    in1=cos3[:, ms, :, :, :].rearrange("p m h j e -> p m (h j e)"),
+                    out=ca[:, ms, :], in0=a[:], in1=cos_n[:, ms, :, :, :].rearrange("p m h j e -> p m (h j e)"), op=MULT
+                )
+                nc.vector.tensor_tensor(
+                    out=sb[:, ms, :].rearrange("p m (q e) -> p m q e", e=2),
+                    in0=a[:].rearrange("p m (q e) -> p m q e", e=2)[:, :, :, ::-1],
+                    in1=sin_n[:, ms, :, :, :].rearrange("p m h j e -> p m (h j) e"),
                     op=MULT,
                 )
                 if mp == 0:
-                    tick()
-                nc.vector.tensor_tensor(
-                    out=tb[:, ms, :, :],
-                    in0=a[:].rearrange("p m (q e) -> p m e q", e=2),
-                    in1=sin3[:, ms, :, :, :].rearrange("p m e h j -> p m e (h j)"),
-                    op=MULT,
-                )
-                if on_pool and mp == 0:
-                    add(nc.gpsimd, 0, 1)
+                    add(nc.gpsimd, 0, own)
 
-            def rest():
-                add(nc.vector, 1 if on_pool else 0, 4)
+            def rest(last):
+                add(nc.vector, own, 512)
+                if last:
+                    store(0, 2)
+                    add(nc.vector, 512, 1024)
+                    store(2, 4)
+                else:
+                    add(nc.gpsimd, 512 - SHARED, 1024)
+                    store(0, 4)
 
             pend.append(rest)
 
@@ -385,6 +405,8 @@ def tile_attention_pa_kernel(
         run = {
             "load": load,
             "dummy": dummy,
+            "spread": spread,
+            "tables": tables,
             "cast": cast,
             "product": product,
             "turn": turn,
@@ -394,7 +416,7 @@ def tile_attention_pa_kernel(
             "mm": mm,
             "rope_pair": rope_pair,
             "evac": evac,
-            "flush": tick,
+            "flush": lambda: tick(True),
         }
         for op in schedule(
             T_ORDER, M_ORDER, SCALED, LEAD, Q_LAG, Q_LAG_SCALED, ROPE_LAG, BURST, POOL_ADDS, WARM0, WARM1, CAST_FROM, LOAD_ORDER, LATE_LOADS, MM_BURST, DEFER, WARM_EVERY, True, Q_LAG_HEAD, LEAD_HEAD

from contextlib import ExitStack

import concourse.mybir as mybir
from concourse.masks import make_identity

F32 = mybir.dt.float32
BF16 = mybir.dt.bfloat16
U8 = mybir.dt.uint8
U32 = mybir.dt.uint32
FP8 = mybir.dt.float8_e4m3fn
FP8X4 = mybir.dt.float8_e4m3fn_x4
MULT = mybir.AluOpType.mult
ADD = mybir.AluOpType.add
COPY = mybir.ActivationFunctionType.Copy

P = 128
E = 2048
PASSES = 4
FLOPS = 2 * 512 * 3072 * 2048

T_ORDER = (0, 24, 1, 25, 2, 26, 3, 27, 4, 5, 6, 7, 16, 17, 12, 13, 18, 19, 8, 9, 14, 15, 20, 21, 22, 23, 10, 11)
M_ORDER = (0, 1, 2, 8, 3, 9, 6, 4, 10, 7, 11, 5)
SCALED = (6, 7)
LEAD = 1
LEAD_HEAD = 2
Q_LAG = 3
Q_LAG_HEAD = 3
Q_LAG_SCALED = 2
ROPE_LAG = 3
BURST = 1
POOL_ADDS = True
POOL_OWN = 256
POOL_LAST = 320
SHARED = 8
WARM0 = 12
WARM_FIRST = 2
TABLE_STEP = 0
WARM1 = 2
WARM_EVERY = 3
CAST_FROM = 6
MM_BURST = 1
MM_LAG_HEAD = 1
MM_HEAD = 4
DEFER = True
LOAD_ORDER = ('sc', 0, 1, 'cs', 2, 24, 3, 25, 4, 26, 5, 6, 27, 7, 12, 13, 16, 8, 17, 9, 14, 15, 18, 10, 19, 11)
LATE_LOADS = (20, 21, 22, 23)


def schedule(t_order, m_order, scaled, lead, q_lag, q_lag_scaled, rope_lag, burst, pool_adds, warm0, warm1, cast_from, load_order, late_loads, mm_burst=1, defer=False, warm_every=1, pair_rope=False, q_lag_head=None, lead_head=None):
    ops = []
    for t in load_order:
        ops.append(("load", t))
    ops.append(("dummy", WARM_FIRST))
    ops.append(("spread",))
    if warm0:
        ops.append(("dummy", warm0))
    banks = [(pr, mp) for pr in m_order for mp in (0, 1)]
    last_turn = {}
    for s, t in enumerate(t_order):
        last_turn[t // 2] = s
    casts = [(t, h) for t in t_order if t // 2 in scaled for h in (0, 1)]
    n_cast = 0
    weaves = []
    n_weave = 0
    products = [t for t in t_order if t < 16 and t // 2 not in scaled]
    n_made = 0
    q_order = [12, m_order[0], 13] + list(m_order[1:])
    n_q = 0
    quantized = {}
    n_mm = 0
    mm_step = {}
    n_rope = 0
    steps = len(t_order)
    s = 0
    while n_rope < len(banks):
        assert s < 200
        want = n_cast + 1 if s >= cast_from else n_cast
        if s < steps and t_order[s] // 2 in scaled:
            want = max(want, 1 + max(i for i in range(len(casts)) if casts[i][0] // 2 == t_order[s] // 2))
        want = min(want, len(casts))
        if n_weave < len(weaves) and n_cast >= want:
            ops.append(("weave",) + weaves[n_weave])
            n_weave += 1
        while n_cast < want:
            ops.append(("cast",) + casts[n_cast])
            n_cast += 1
        turned = len([t for t in products if t in t_order[: s + 1]])
        ahead = lead_head if (lead_head is not None and n_mm == 0) else lead
        while n_made < min(turned + ahead, len(products)):
            ops.append(("product", products[n_made], 1 if n_made else 4))
            n_made += 1
        if s == TABLE_STEP:
            ops.append(("tables",))
        if s < steps:
            t = t_order[s]
            if t // 2 in scaled:
                for g in (2 * (t % 2), 2 * (t % 2) + 1):
                    ops.append(("turn_scaled", t // 2, g))
                    if defer:
                        weaves.append((t // 2, g))
                    else:
                        ops.append(("weave", t // 2, g))
            else:
                ops.append(("turn", t))
                if t == 27:
                    for late in late_loads:
                        ops.append(("load", late))
            if warm1 and n_mm == 0 and s % warm_every == warm_every - 1:
                ops.append(("dummy", warm1))
        due = [b for b in range(n_rope, n_mm) if mm_step[b] + rope_lag <= s]
        if pair_rope:
            while len(due) >= 2:
                pr = banks[due[0]][0]
                if pr >= 10:
                    ops.append(("evac", pr, 0))
                    ops.append(("evac", pr, 1))
                else:
                    ops.append(("rope_pair", pr, pool_adds))
                n_rope += 2
                due = due[2:]
        elif len(due) >= burst or (n_mm == len(banks) and due):
            for b in due:
                pr, mp = banks[b]
                if pr >= 10:
                    ops.append(("evac", pr, mp))
                else:
                    ops.append(("rope", pr, mp, pool_adds and b != due[-1]))
                n_rope += 1
        if n_q < len(q_order):
            pr = q_order[n_q]
            lag = q_lag_scaled if pr in scaled else q_lag
            if q_lag_head is not None and n_q < 3:
                lag = q_lag_head
            if last_turn[pr] + lag <= s and (pr, 3) not in weaves[n_weave:]:
                ops.append(("quantize", pr))
                quantized[pr] = s
                n_q += 1
        ready = 0
        while n_mm + ready < len(banks) and ready < mm_burst:
            pr, mp = banks[n_mm + ready]
            wait = MM_LAG_HEAD if n_mm + ready < MM_HEAD else 0
            if quantized.get(pr, 999) + wait <= s and quantized.get(12 + mp, 999) + wait <= s and n_rope > n_mm + ready - 4:
                ready += 1
            else:
                break
        if ready == mm_burst or (s >= steps and ready) or n_mm + ready == len(banks):
            for i in range(ready):
                ops.append(("mm",) + banks[n_mm])
                mm_step[n_mm] = s
                n_mm += 1
        s += 1
    ops.append(("flush",))
    return ops


def tile_attention_pa_kernel(
    tc, x, wq_w_bytes, wq_w_scale, wk_w, wv_w, freqs_cos, freqs_sin, out_0, out_1, out_2
):
    nc = tc.nc
    x_rows = x.flatten_outer_dims()
    out_views = (
        out_0.rearrange("b (m p) h d -> p (b m) (h d)", p=P),
        out_1.rearrange("b (m p) h d -> p (b m) (h d)", p=P),
        out_2.rearrange("b (m p) h d -> p (b m) (h d)", p=P),
    )

    with ExitStack() as ctx:
        const = ctx.enter_context(tc.tile_pool(name="const", bufs=1))
        bytes_pool = ctx.enter_context(tc.tile_pool(name="bytesp", bufs=1))
        raw = ctx.enter_context(tc.tile_pool(name="raw", bufs=1))
        wbf_pool = ctx.enter_context(tc.tile_pool(name="wbfp", bufs=max(LEAD, LEAD_HEAD) + 3))
        plane_pool = ctx.enter_context(tc.tile_pool(name="planep", bufs=5))
        grp_pool = ctx.enter_context(tc.tile_pool(name="grpp", bufs=5))
        code_pool = ctx.enter_context(tc.tile_pool(name="codep", bufs=1))
        work = ctx.enter_context(tc.tile_pool(name="work", bufs=2))
        psum = ctx.enter_context(tc.psum_pool(name="psum", bufs=1))
        ctx.enter_context(tc.manual_schedule())

        zeros = const.tile([P, 512], BF16, name="zeros")
        nc.vector.memset(zeros[:], 0.0)
        warm = const.tile([P, 2], F32, name="warm")
        nc.vector.memset(warm[:, 0:1], 0.0)
        nc.scalar.activation(out=warm[:, 1:2], in_=warm[:, 0:1], func=COPY, scale=1.0)
        ident = const.tile([P, P], F32, name="ident")
        make_identity(nc, ident[:])

        scale_bc = const.tile([P, E], F32, name="scale_bc")
        scale_col = const.tile([P, PASSES, 4], F32, name="scale_col")
        cos_t = const.tile([P, 4, 64], BF16, name="cos_t")
        sin_t = const.tile([P, 4, 64], BF16, name="sin_t")
        cos_n = const.tile([P, 4, 2, 64, 2], BF16, name="cos_n")
        sin_n = const.tile([P, 4, 2, 64, 2], BF16, name="sin_n")
        wq_codes_in = {}
        words = {}

        def load(t):
            if t == "sc":
                nc.sync.dma_start(out=scale_col[:], in_=wq_w_scale.rearrange("o (g p t) -> p (o g) t", p=P, t=4))
            elif t == "cs":
                nc.sync.dma_start(out=cos_t[:], in_=freqs_cos.rearrange("(m p) j -> p m j", p=P))
                nc.sync.dma_start(out=sin_t[:], in_=freqs_sin.rearrange("(m p) j -> p m j", p=P))
            elif t < 16:
                b = bytes_pool.tile([P, E], U8, name="wq_bytes_%d" % t)
                nc.sync.dma_start(out=b[:], in_=wq_w_bytes[t * P : (t + 1) * P, :])
                wq_codes_in[t] = b
            else:
                src = (wk_w, wv_w, x_rows)[(t - 16) // 4]
                j = t % 4
                rows = raw.tile([P, E], BF16, name="rows_%d" % t, tag=("rk%d" % j) if t < 20 else ("rx%d" % j))
                nc.sync.dma_start(out=rows[:], in_=src[j * P : (j + 1) * P, :])
                words[t] = rows[:].bitcast(F32)

        def tables():
            for h in range(2):
                nc.scalar.copy(out=cos_n[:, :, h, :, :], in_=cos_t[:].unsqueeze(3).to_broadcast([P, 4, 64, 2]))
                nc.scalar.activation(out=sin_n[:, :, h, :, 0], in_=sin_t[:], func=COPY, scale=-1.0)
                nc.scalar.copy(out=sin_n[:, :, h, :, 1], in_=sin_t[:])

        pend = []
        flushed = [0]

        def tick(last):
            if flushed[0] < len(pend):
                flushed[0] = flushed[0] + 1
                pend[flushed[0] - 1](last)

        dummy_out = []

        def dummy(n):
            if not dummy_out:
                dummy_out.append(psum.tile([P, 512], F32, name="dummy_out", tag="b3"))
            for i in range(n):
                nc.tensor.matmul(dummy_out[0][:], lhsT=zeros[:, 0:P], rhs=zeros[:], start=True, stop=True)

        def product(t, chunks):
            w = wbf_pool.tile([P, E], BF16, name="wbf_%d" % t, tag="wbf")
            n = E // chunks
            for c in range(chunks):
                cs = slice(c * n, (c + 1) * n)
                nc.vector.tensor_tensor(
                    out=w[:, cs], in0=wq_codes_in[t][:, cs].bitcast(FP8), in1=scale_bc[:, cs], op=MULT
                )
            words[t] = w[:].bitcast(F32)

        cast_tiles = {}

        def cast(t, h):
            if t not in cast_tiles:
                cast_tiles[t] = raw.tile([P, E], BF16, name="wcast_%d" % t)
                words[t] = cast_tiles[t][:].bitcast(F32)
            cs = slice(h * 1024, (h + 1) * 1024)
            nc.scalar.copy(out=cast_tiles[t][:, cs], in_=wq_codes_in[t][:, cs].bitcast(FP8))

        grp = {}
        n_tbank = [0]

        def tbank(shape, name):
            n_tbank[0] = n_tbank[0] + 1
            return psum.tile(shape, F32, name=name, tag="b%d" % (4 + (n_tbank[0] - 1) % 4))

        def grp_tile(pair):
            if pair not in grp:
                grp[pair] = grp_pool.tile([P, PASSES, 2 * P, 4], BF16, name="grp_%d" % pair, tag="grp", align_bytes=64)
            return grp[pair]

        def turn(t):
            pair, i = t // 2, t % 2
            grp_words = grp_tile(pair)[:].bitcast(F32)
            for gg in range(2):
                tp = tbank([P, 2, 2, P], "tp_%d_%d" % (t, gg))
                for g2 in range(2):
                    g = 2 * gg + g2
                    for u in range(2):
                        nc.tensor.transpose(tp[:, g2, u, :], words[t][:, 256 * g + u : 256 * (g + 1) : 2], ident[:])
                nc.scalar.copy(
                    out=grp_words[:, 2 * gg : 2 * gg + 2, i * P : (i + 1) * P, :],
                    in_=tp[:].rearrange("p g u r -> p g r u"),
                )

        def spread():
            for g in range(PASSES):
                sp = tbank([P, 4, P], "spread_%d" % g)
                for t in range(4):
                    nc.tensor.transpose(sp[:, t, :], scale_col[:, g, t : t + 1].to_broadcast([P, P]), ident[:])
                nc.scalar.copy(
                    out=scale_bc[:, g * 512 : (g + 1) * 512].rearrange("p (n t) -> p n t", t=4),
                    in_=sp[:].rearrange("p t n -> p n t"),
                )

        plane_tiles = {}

        def turn_scaled(pair, g):
            grp_tile(pair)
            tp = tbank([P, 2, 2 * P], "tps_%d_%d" % (pair, g))
            for i in range(2):
                for u in range(2):
                    nc.tensor.transpose(
                        tp[:, u, i * P : (i + 1) * P], words[2 * pair + i][:, 256 * g + u : 256 * (g + 1) : 2], ident[:]
                    )
            halves = tp[:].rearrange("p u c -> p (u c)").bitcast(BF16).rearrange("p (u c e) -> p u c e", u=2, e=2)
            planes = plane_pool.tile([P, 4, 2 * P], BF16, name="planes_%d_%d" % (pair, g), tag="planes")
            for t in range(4):
                nc.scalar.activation(
                    out=planes[:, t, :], in_=halves[:, t // 2, :, t % 2], func=COPY, scale=scale_col[:, g, t : t + 1]
                )
            plane_tiles[(pair, g)] = planes

        def weave(pair, g):
            nc.scalar.copy(out=grp[pair][:, g, :, :], in_=plane_tiles[(pair, g)][:].rearrange("p t c -> p c t"))

        codes = {}
        scales = {}

        def quantize(pair):
            if pair < 12:
                c = code_pool.tile([P, 1024], U32, name="codes_%d" % pair, tag="wc", bufs=4, align_bytes=64)
                s = code_pool.tile([P, 1024], U8, name="scales_%d" % pair, tag="ws", bufs=4, align_bytes=64)
            else:
                c = code_pool.tile([P, 1024], U32, name="codes_%d" % pair, align_bytes=64)
                s = code_pool.tile([P, 1024], U8, name="scales_%d" % pair, align_bytes=64)
            nc.vector.quantize_mx(
                out=c[:].bitcast(FP8X4), scales=s[:], in_=grp[pair][:].rearrange("p g c t -> p (g c t)")
            )
            codes[pair] = c
            scales[pair] = s

        acc = {}
        n_acc = [0]

        def mm(pair, mp):
            a = psum.tile([P, 2, 256], F32, name="acc_%d_%d" % (pair, mp), tag="b%d" % (n_acc[0] % 4))
            n_acc[0] = n_acc[0] + 1
            acc[(pair, mp)] = a
            for mh in range(2):
                for g in range(PASSES):
                    xs = slice(g * 256 + mh * P, g * 256 + mh * P + P)
                    ws = slice(g * 256, (g + 1) * 256)
                    nc.tensor.matmul_mx(
                        out=a[:, mh, :],
                        lhsT=codes[12 + mp][:, xs].bitcast(FP8X4),
                        lhsT_scale=scales[12 + mp][:, xs],
                        rhs=codes[pair][:, ws].bitcast(FP8X4),
                        rhs_scale=scales[pair][:, ws],
                        start=(g == 0),
                        stop=(g == PASSES - 1),
                    )

        def store(pair, mp, tile2):
            view = out_views[0] if pair < 8 else out_views[1] if pair < 10 else out_views[2]
            col = (pair if pair < 8 else pair % 2) * 256
            nc.sync.dma_start(out=view[:, 2 * mp : 2 * mp + 2, col : col + 256], in_=tile2)

        def rope_pair(pair, on_pool):
            tick(False)
            own = POOL_LAST if pair == [pr for pr in M_ORDER if pr < 10][-1] else POOL_OWN
            ca = work.tile([P, 4, 256], F32, name="ca_%d" % pair, tag="ca")
            sb = work.tile([P, 4, 256], F32, name="sb_%d" % pair, tag="sb")
            r = work.tile([P, 4, 256], F32, name="r_%d" % pair, tag="r", bufs=3)
            view = out_views[0] if pair < 8 else out_views[1]
            col = (pair if pair < 8 else pair % 2) * 256

            def add(eng, c0, c1):
                eng.tensor_tensor(
                    out=r[:].rearrange("p m c -> p (m c)")[:, c0:c1],
                    in0=ca[:].rearrange("p m c -> p (m c)")[:, c0:c1],
                    in1=sb[:].rearrange("p m c -> p (m c)")[:, c0:c1],
                    op=ADD,
                )

            def store(m0, m1):
                nc.sync.dma_start(out=view[:, m0:m1, col : col + 256], in_=r[:, m0:m1, :])

            for mp in range(2):
                a = acc[(pair, mp)]
                ms = slice(2 * mp, 2 * mp + 2)
                nc.vector.tensor_tensor(
                    out=ca[:, ms, :], in0=a[:], in1=cos_n[:, ms, :, :, :].rearrange("p m h j e -> p m (h j e)"), op=MULT
                )
                nc.vector.tensor_tensor(
                    out=sb[:, ms, :].rearrange("p m (q e) -> p m q e", e=2),
                    in0=a[:].rearrange("p m (q e) -> p m q e", e=2)[:, :, :, ::-1],
                    in1=sin_n[:, ms, :, :, :].rearrange("p m h j e -> p m (h j) e"),
                    op=MULT,
                )
                if mp == 0:
                    add(nc.gpsimd, 0, own)

            def rest(last):
                add(nc.vector, own, 512)
                if last:
                    store(0, 2)
                    add(nc.vector, 512, 1024)
                    store(2, 4)
                else:
                    add(nc.gpsimd, 512 - SHARED, 1024)
                    store(0, 4)

            pend.append(rest)

        def evac(pair, mp):
            vt = work.tile([P, 2, 256], F32, name="vt_%d_%d" % (pair, mp), tag="vt")
            nc.scalar.copy(out=vt[:], in_=acc[(pair, mp)][:])
            store(pair, mp, vt[:])

        run = {
            "load": load,
            "dummy": dummy,
            "spread": spread,
            "tables": tables,
            "cast": cast,
            "product": product,
            "turn": turn,
            "turn_scaled": turn_scaled,
            "weave": weave,
            "quantize": quantize,
            "mm": mm,
            "rope_pair": rope_pair,
            "evac": evac,
            "flush": lambda: tick(True),
        }
        for op in schedule(
            T_ORDER, M_ORDER, SCALED, LEAD, Q_LAG, Q_LAG_SCALED, ROPE_LAG, BURST, POOL_ADDS, WARM0, WARM1, CAST_FROM, LOAD_ORDER, LATE_LOADS, MM_BURST, DEFER, WARM_EVERY, True, Q_LAG_HEAD, LEAD_HEAD
        ):
            run[op[0]](*op[1:])
